import numpy as np
import ml_dtypes


def mxq(x, axis, fmt="e4m3"):
    dtype, down = {"e4m3": (ml_dtypes.float8_e4m3fn, 7), "e5m2": (ml_dtypes.float8_e5m2, 14)}[fmt]
    v = np.moveaxis(np.asarray(x, np.float32).astype(ml_dtypes.bfloat16).astype(np.float64), axis, -1)
    blocks = v.reshape(v.shape[:-1] + (-1, 32))
    amax = np.abs(blocks).max(-1, keepdims=True)
    byte = np.maximum(np.where(amax > 0, np.frexp(amax)[1] - 1 + 127, 0) - down, 1)
    scale = np.exp2(byte - 127.0)
    codes = (blocks / scale).astype(np.float32).astype(dtype).astype(np.float64)
    return np.moveaxis((codes * scale).reshape(v.shape), -1, axis)


WIDE = False


def mx_kscale(k):
    if not WIDE:
        return np.ones(k)
    levels = np.array([10, -10, 5, -5, 0])
    a = np.random.permutation(np.resize(levels, k // 512 * 4)).reshape(k // 512, 4)
    idx = np.arange(k)
    return np.exp2(a[idx // 512, idx % 128 // 32])


BF16 = ml_dtypes.bfloat16


def bf(x):
    return np.asarray(x, np.float32).astype(BF16)


def f64(x):
    return np.asarray(x).astype(np.float64)


N, CIN, COUT, V, T, S = 2, 1024, 64, 64, 64, 8
EPS = 1e-5
KG = S * V


def setup_inputs():
    r = np.random.standard_normal
    c = mx_kscale(CIN)
    g = mx_kscale(KG).reshape(S, V)
    return {"ada_A": bf(r((N, CIN, V, V)) * c[None, :, None, None]),
            "ada_w": bf(r((S, COUT, CIN)) / np.sqrt(CIN) / c),
            "ada_b": bf(r((S, COUT)) * 0.3),
            "PA": bf(r((S, V, V)) * 2.0 / np.sqrt(KG) * g[:, None, :]),
            "feat": bf(r((S, N, COUT, V, T)) / g[:, None, None, :, None]),
            "bn_gamma": bf(1.0 + 0.1 * r(COUT)),
            "bn_beta": bf(0.3 * r(COUT)),
            "bn_mean": bf(0.3 * r(COUT)),
            "bn_var": bf(np.abs(r(COUT)) + 1.0),
            "res": bf(r((N, COUT, V, T)) * 0.9)}


def reference(ada_A, ada_w, ada_b, PA, feat, bn_gamma, bn_beta, bn_mean, bn_var, res):
    wq = mxq(f64(ada_w).reshape(S * COUT, CIN), 1, "e4m3")
    aq = mxq(f64(ada_A).reshape(N, CIN, V * V), 1, "e4m3")
    adaA = (wq @ aq).reshape(N, S, COUT, V, V).transpose(1, 0, 2, 3, 4) + f64(ada_b)[:, None, :, None, None]
    A_full = adaA * f64(PA)[:, None, None, :, :]
    Ag = A_full.transpose(1, 2, 3, 0, 4).reshape(N, COUT, V, KG)
    Fg = f64(feat).transpose(1, 2, 0, 3, 4).reshape(N, COUT, KG, T)
    y = mxq(Ag, 3, "e4m3") @ mxq(Fg, 2, "e4m3")
    scale = f64(bn_gamma) / np.sqrt(f64(bn_var) + EPS)
    z = (y - f64(bn_mean)[:, None, None]) * scale[:, None, None] + f64(bn_beta)[:, None, None]
    return np.maximum(z + f64(res), 0.0)

@@ -1,0 +1,375 @@
+from contextlib import ExitStack
+
+import concourse.mybir as mybir
+from concourse.masks import make_identity
+
+F32 = mybir.dt.float32
+BF16 = mybir.dt.bfloat16
+U32 = mybir.dt.uint32
+U8 = mybir.dt.uint8
+FP8X4 = mybir.dt.float8_e4m3fn_x4
+ACT = mybir.ActivationFunctionType
+ALU = mybir.AluOpType
+
+N, CIN, COUT, V, T, S = 2, 1024, 64, 64, 64, 8
+EPS = 1e-5
+FLOPS = 2 * N * S * COUT * CIN * V * V + 2 * N * COUT * V * S * V * T
+
+P = 128
+PACK = 4
+K_PASS = P * PACK
+C_PASSES = CIN // K_PASS
+SG = 4
+SX = 2
+WQ = V // 2
+A_COLS = 1024
+A_TILES = N * C_PASSES * V * V // A_COLS
+CHUNK = 512
+V_CHUNK = CHUNK // V
+CHUNKS = N * V * V // CHUNK
+CHUNKS_N = CHUNKS // N
+O_BANK = 8
+BANKS_N = COUT // O_BANK
+O_LOAD = 32
+AHEAD = 2
+VECTOR_COLS = 448
+VECTOR_CHANNELS = 4
+F_LIVE = BANKS_N + 1
+
+
+def tile_multiscale_gcn_pa_t_kernel(
+    tc, ada_A, ada_w, ada_b, PA, feat, bn_gamma, bn_beta, bn_mean, bn_var, res, out
+):
+    nc = tc.nc
+    with ExitStack() as ctx:
+        const = ctx.enter_context(tc.tile_pool(name="const", bufs=1))
+        raw_pool = ctx.enter_context(tc.tile_pool(name="raw", bufs=4))
+        grouped_pool = ctx.enter_context(tc.tile_pool(name="grouped", bufs=2))
+        code_pool = ctx.enter_context(tc.tile_pool(name="codes", bufs=2))
+        x_pool = ctx.enter_context(tc.tile_pool(name="x", bufs=2))
+        a_pool = ctx.enter_context(tc.tile_pool(name="a", bufs=1))
+        f_raw_pool = ctx.enter_context(tc.tile_pool(name="f_raw", bufs=2))
+        f_code_pool = ctx.enter_context(tc.tile_pool(name="f_codes", bufs=F_LIVE))
+        z_pool = ctx.enter_context(tc.tile_pool(name="z", bufs=4))
+        ps_mx = ctx.enter_context(tc.psum_pool(name="ps_mx", bufs=4))
+        ps_turn = ctx.enter_context(tc.psum_pool(name="ps_turn", bufs=4))
+        ctx.enter_context(tc.manual_schedule())
+
+        def load_ada(index):
+            quarter, c = divmod(index, C_PASSES)
+            n, q = divmod(quarter, V * V // A_COLS)
+            v0 = q * (A_COLS // V)
+            raw = raw_pool.tile([P, PACK, A_COLS], BF16, tag="raw")
+            nc.sync.dma_start(
+                out=raw[:],
+                in_=ada_A[
+                    n, K_PASS * c : K_PASS * (c + 1), v0 : v0 + A_COLS // V, :
+                ].rearrange("(p j) v w -> p j (v w)", j=PACK),
+            )
+            return raw
+
+        def load_feat(n, first_o):
+            f_raw = f_raw_pool.tile([P, O_LOAD, SX, 2 * T], BF16)
+            for g in range(SG):
+                for x in range(SX):
+                    nc.sync.dma_start(
+                        out=f_raw[WQ * g : WQ * (g + 1), :, x, :],
+                        in_=feat[g + SG * x, n, first_o : first_o + O_LOAD, :, :].rearrange(
+                            "o (q e) t -> q o (e t)", e=2
+                        ),
+                    )
+            return f_raw
+
+        raws = {0: load_ada(0)}
+        w_raw = raw_pool.tile([P, SG, CIN], BF16, tag="raw")
+        for x in range(SX):
+            nc.sync.dma_start(
+                out=w_raw[COUT * x : COUT * (x + 1), :, :],
+                in_=ada_w[SG * x : SG * (x + 1)].rearrange("g o i -> o g i"),
+            )
+        raws[1] = load_ada(1)
+        f_raws = {}
+
+        b_raw = const.tile([SG, SX * COUT], BF16)
+        nc.scalar.dma_start(
+            out=b_raw[:].rearrange("g (x o) -> g x o", x=SX),
+            in_=ada_b.rearrange("(x g) o -> g x o", x=SX),
+        )
+        pa_raw = const.tile([P, SG * V], BF16)
+        for x in range(SX):
+            nc.scalar.dma_start(
+                out=pa_raw[V * x : V * (x + 1), :].rearrange("v (g w) -> v g w", g=SG),
+                in_=PA[SG * x : SG * (x + 1)].rearrange("g v w -> v g w"),
+            )
+        bn_raw = const.tile([P, 4, COUT], BF16)
+        for i, vec in enumerate((bn_gamma, bn_beta, bn_mean, bn_var)):
+            nc.scalar.dma_start(out=bn_raw[:, i, :], in_=vec.partition_broadcast(P))
+        res_sb = const.tile([P, N * COUT // 2, T], BF16)
+        nc.gpsimd.dma_start(
+            out=res_sb[:], in_=res.rearrange("n (a h) v t -> (h v) (n a) t", h=2)
+        )
+        out_view = out.rearrange("n (a h) v t -> (h v) n a t", h=2)
+
+        ident = const.tile([P, P], F32)
+        make_identity(nc, ident[:])
+
+        def regroup_ada(raw):
+            grouped = grouped_pool.tile([P, A_COLS, PACK], BF16, tag="grouped", align_bytes=64)
+            dst = grouped[:].rearrange("p (c i) j -> p c j i", i=4)
+            src = raw[:].rearrange("p j (c i) -> p c j i", i=4)
+            cut = VECTOR_COLS // 4
+            nc.vector.tensor_copy(out=dst[:, :cut], in_=src[:, :cut])
+            nc.scalar.copy(out=dst[:, cut:], in_=src[:, cut:])
+            return grouped
+
+        def regroup_feat(f_raw, first_o):
+            f_grouped = grouped_pool.tile([P, O_BANK * T, PACK], BF16, align_bytes=64)
+            dst = f_grouped[:].rearrange("p (o t) j -> p o t j", t=T)
+            src = f_raw[:, first_o : first_o + O_BANK, :, :].rearrange(
+                "p o x (e t) -> p o t (x e)", e=2
+            )
+            cut = VECTOR_CHANNELS
+            nc.vector.tensor_copy(out=dst[:, :cut], in_=src[:, :cut])
+            nc.scalar.copy(out=dst[:, cut:], in_=src[:, cut:])
+            return f_grouped
+
+        def quantise(grouped, codes, scales):
+            nc.vector.quantize_mx(
+                out=codes.bitcast(FP8X4),
+                scales=scales,
+                in_=grouped[:].rearrange("p w j -> p (w j)"),
+            )
+
+        a_code_tiles = {}
+        f_code_tiles = {}
+
+        def quantise_ada(index, grouped):
+            quarter, c = divmod(index, C_PASSES)
+            if c == 0:
+                a_codes = code_pool.tile([P, C_PASSES, A_COLS], U32, align_bytes=64)
+                a_scales = code_pool.tile([P, C_PASSES, A_COLS], U8, align_bytes=64)
+                a_code_tiles[quarter] = (a_codes, a_scales)
+            a_codes, a_scales = a_code_tiles[quarter]
+            quantise(grouped, a_codes[:, c, :], a_scales[:, c, :])
+
+        def prepare_feat(group):
+            per_load = O_LOAD // O_BANK
+            if group % per_load == 0:
+                n, bank = divmod(group, BANKS_N)
+                f_raws[group // per_load] = load_feat(n, O_BANK * bank)
+            return regroup_feat(f_raws[group // per_load], O_BANK * (group % per_load))
+
+        def quantise_feat(group, f_grouped):
+            f_codes = f_code_pool.tile([P, O_BANK * T], U32, align_bytes=64)
+            f_scales = f_code_pool.tile([P, O_BANK * T], U8, align_bytes=64)
+            quantise(f_grouped, f_codes[:], f_scales[:])
+            f_code_tiles[group] = (f_codes, f_scales)
+
+        grouped_0 = regroup_ada(raws[0])
+
+        w_words = w_raw[:].bitcast(F32).rearrange("m g (c p u) -> m g c u p", c=C_PASSES, u=2)
+        w_grouped = grouped_pool.tile([P, A_COLS, PACK], BF16, tag="grouped", align_bytes=64)
+        w_grouped_words = (
+            w_grouped[:]
+            .rearrange("p w j -> p (w j)")
+            .bitcast(F32)
+            .rearrange("p (c g m u) -> p c g m u", c=C_PASSES, g=SG, u=2)
+        )
+        for c in range(C_PASSES):
+            for g_pair in range(SG // 2):
+                w_turned = ps_turn.tile([P, 4, P], F32, tag="turned")
+                for g_low in range(2):
+                    for u in range(2):
+                        nc.tensor.transpose(
+                            w_turned[:, 2 * g_low + u, :],
+                            w_words[:, 2 * g_pair + g_low, c, u, :],
+                            ident[:],
+                        )
+                copy_out = nc.vector.tensor_copy if g_pair == 0 else nc.scalar.copy
+                copy_out(
+                    out=w_grouped_words[:, c, 2 * g_pair : 2 * g_pair + 2, :, :],
+                    in_=w_turned[:].rearrange("p (g u) m -> p g m u", u=2),
+                )
+        w_codes = const.tile([P, C_PASSES * SG * P], U32, align_bytes=64)
+        w_scales = const.tile([P, C_PASSES * SG * P], U8, align_bytes=64)
+
+        b_square = const.tile([P, P], F32)
+        nc.vector.memset(b_square[:], 0.0)
+        nc.vector.tensor_copy(out=b_square[0:SG, :], in_=b_raw[:])
+        b_turned = ps_turn.tile([P, 4, P], F32, tag="turned")
+        nc.tensor.transpose(b_turned[:, 0, :], b_square[:], ident[:])
+        bias_col = const.tile([P, SG], F32)
+        nc.vector.tensor_copy(out=bias_col[:], in_=b_turned[:, 0, 0:SG])
+
+        quantise(w_grouped, w_codes[:], w_scales[:])
+        quantise_ada(0, grouped_0)
+        grouped_1 = regroup_ada(raws[1])
+
+        pa_sorted = const.tile([P, 2, P], F32)
+        nc.vector.tensor_copy(out=pa_sorted[:], in_=pa_raw[:].rearrange("p (k e) -> p e k", e=2))
+        pa_turned = ps_turn.tile([P, 4, P], F32, tag="turned")
+        for e in range(2):
+            nc.tensor.transpose(pa_turned[:, e, :], pa_sorted[:, e, :], ident[:])
+        pa_t = const.tile([P, V, PACK], F32)
+        nc.vector.tensor_copy(
+            out=pa_t[:].rearrange("p v (x e) -> p v x e", x=SX),
+            in_=pa_turned[:, 0:2, :].rearrange("p e (x v) -> p v x e", x=SX),
+        )
+
+        quantise_ada(1, grouped_1)
+
+        bn_f = const.tile([P, 4, COUT], F32)
+        nc.vector.tensor_copy(out=bn_f[:], in_=bn_raw[:])
+        rstd = const.tile([P, COUT], F32)
+        nc.vector.tensor_scalar_add(out=rstd[:], in0=bn_f[:, 3, :], scalar1=EPS)
+        nc.scalar.activation(out=rstd[:], in_=rstd[:], func=ACT.Sqrt)
+        nc.vector.reciprocal(out=rstd[:], in_=rstd[:])
+        scale_all = const.tile([P, COUT], F32)
+        nc.vector.tensor_mul(out=scale_all[:], in0=bn_f[:, 0, :], in1=rstd[:])
+        shift_all = const.tile([P, COUT], F32)
+        nc.vector.tensor_mul(out=shift_all[:], in0=bn_f[:, 2, :], in1=scale_all[:])
+        nc.vector.tensor_sub(out=shift_all[:], in0=bn_f[:, 1, :], in1=shift_all[:])
+        scale_col = const.tile([P, COUT // 2], F32)
+        shift_col = const.tile([P, COUT // 2], F32)
+        for h in range(2):
+            rows = slice(V * h, V * (h + 1))
+            nc.vector.tensor_copy(
+                out=scale_col[rows, :],
+                in_=scale_all[rows, :].rearrange("p (a h) -> p h a", h=2)[:, h, :],
+            )
+            nc.vector.tensor_copy(
+                out=shift_col[rows, :],
+                in_=shift_all[rows, :].rearrange("p (a h) -> p h a", h=2)[:, h, :],
+            )
+
+        def first_matmul(chunk):
+            a_codes, a_scales = a_code_tiles[chunk // 2]
+            cols = slice(CHUNK * (chunk % 2), CHUNK * (chunk % 2 + 1))
+            x_sb = x_pool.tile([P, V_CHUNK, 2, SG, WQ], F32)
+            for g in range(SG):
+                acc = ps_mx.tile([P, CHUNK], F32, tag="mx")
+                for c in range(C_PASSES):
+                    w_cols = slice(P * (SG * c + g), P * (SG * c + g + 1))
+                    nc.tensor.matmul_mx(
+                        out=acc[:],
+                        lhsT=w_codes[:, w_cols].bitcast(FP8X4),
+                        lhsT_scale=w_scales[:, w_cols],
+                        rhs=a_codes[:, c, cols].bitcast(FP8X4),
+                        rhs_scale=a_scales[:, c, cols],
+                        start=(c == 0),
+                        stop=(c == C_PASSES - 1),
+                    )
+                nc.scalar.activation(
+                    out=x_sb[:, :, :, g, :],
+                    in_=acc[:].rearrange("p (v q e) -> p v e q", v=V_CHUNK, e=2),
+                    func=ACT.Identity,
+                    bias=bias_col[:, g : g + 1],
+                    scale=1.0,
+                )
+            return x_sb
+
+        def turn_and_modulate(x_sb, a_in, first_v):
+            for pair in range(V_CHUNK // 2):
+                turned = ps_turn.tile([P, 2, SX, 2, COUT], F32, tag="turned")
+                for dv in range(2):
+                    for e in range(2):
+                        nc.tensor.transpose(
+                            turned[:, dv, :, e, :],
+                            x_sb[:, 2 * pair + dv, e, :, :].rearrange("p g q -> p (g q)"),
+                            ident[:],
+                        )
+                v0 = first_v + 2 * pair
+                nc.vector.tensor_tensor(
+                    out=a_in[:, :, v0 : v0 + 2, :],
+                    in0=turned[:].rearrange("p v x e o -> p o v (x e)"),
+                    in1=pa_t[:, v0 : v0 + 2, :].unsqueeze(1).to_broadcast([P, COUT, 2, PACK]),
+                    op=ALU.mult,
+                )
+
+        def quantise_a(a_in):
+            a_codes2 = a_pool.tile([P, COUT * V], U32, align_bytes=64)
+            a_scales2 = a_pool.tile([P, COUT * V], U8, align_bytes=64)
+            width = O_BANK * V
+            for bank in range(BANKS_N):
+                nc.vector.quantize_mx(
+                    out=a_codes2[:, width * bank : width * (bank + 1)].bitcast(FP8X4),
+                    scales=a_scales2[:, width * bank : width * (bank + 1)],
+                    in_=a_in[:, O_BANK * bank : O_BANK * (bank + 1), :, :].rearrange(
+                        "p o v j -> p (o v j)"
+                    ),
+                )
+            return a_codes2, a_scales2
+
+        def second_matmul(n, bank, a_codes2, a_scales2):
+            f_codes, f_scales = f_code_tiles[BANKS_N * n + bank]
+            y_ps = ps_mx.tile([P, O_BANK // 2, P], F32, tag="mx")
+            z = z_pool.tile([P, O_BANK // 2, T], F32)
+            for pair in range(O_BANK // 2):
+                a = (O_BANK // 2) * bank + pair
+                nc.tensor.matmul_mx(
+                    out=y_ps[:, pair, :],
+                    lhsT=a_codes2[:, P * a : P * (a + 1)].bitcast(FP8X4),
+                    lhsT_scale=a_scales2[:, P * a : P * (a + 1)],
+                    rhs=f_codes[:, P * pair : P * (pair + 1)].bitcast(FP8X4),
+                    rhs_scale=f_scales[:, P * pair : P * (pair + 1)],
+                    start=True,
+                    stop=True,
+                )
+            for pair in range(O_BANK // 2):
+                a = (O_BANK // 2) * bank + pair
+                for h in range(2):
+                    rows = slice(V * h, V * (h + 1))
+                    nc.scalar.activation(
+                        out=z[rows, pair, :],
+                        in_=y_ps[rows, pair, T * h : T * (h + 1)],
+                        func=ACT.Identity,
+                        bias=shift_col[rows, a : a + 1],
+                        scale=scale_col[rows, a : a + 1],
+                    )
+            return z
+
+        def finish(n, bank, z):
+            a0 = (O_BANK // 2) * bank
+            nc.vector.tensor_add(
+                out=z[:],
+                in0=z[:],
+                in1=res_sb[:, (COUT // 2) * n + a0 : (COUT // 2) * n + a0 + O_BANK // 2, :],
+            )
+            nc.vector.tensor_scalar_max(out=z[:], in0=z[:], scalar1=0.0)
+            queue = nc.gpsimd if n == 0 else nc.sync
+            queue.dma_start(out=out_view[:, n, a0 : a0 + O_BANK // 2, :], in_=z[:])
+
+        x_before = None
+        unfinished = None
+        for k in range(CHUNKS + 1):
+            coming = k + AHEAD
+            if coming < A_TILES:
+                raws[coming] = load_ada(coming)
+                grouped = regroup_ada(raws[coming])
+            if k < N * BANKS_N:
+                f_grouped = prepare_feat(k)
+            if unfinished is not None:
+                finish(0, k - CHUNKS_N - 1, unfinished)
+                unfinished = None
+            if k > 0:
+                n, chunk = divmod(k - 1, CHUNKS_N)
+                if chunk == 0:
+                    a_in = a_pool.tile([P, COUT, V, PACK], BF16, align_bytes=64)
+                turn_and_modulate(x_before, a_in, V_CHUNK * chunk)
+                if chunk == CHUNKS_N - 1:
+                    a_codes2, a_scales2 = quantise_a(a_in)
+            if k < CHUNKS:
+                x_before = first_matmul(k)
+            if CHUNKS_N <= k < CHUNKS:
+                unfinished = second_matmul(0, k - CHUNKS_N, a_codes2, a_scales2)
+            if coming < A_TILES:
+                quantise_ada(coming, grouped)
+            if k < N * BANKS_N:
+                quantise_feat(k, f_grouped)
+
+        for bank in range(BANKS_N):
+            z = second_matmul(1, bank, a_codes2, a_scales2)
+            if bank > 0:
+                finish(1, bank - 1, unfinished)
+            unfinished = z
+        finish(1, BANKS_N - 1, unfinished)

@@ -32,6 +32,7 @@ O_BANK = 8
 BANKS_N = COUT // O_BANK
 O_LOAD = 32
 AHEAD = 2
+EARLY = 2
 VECTOR_COLS = 448
 VECTOR_CHANNELS = 4
 F_LIVE = BANKS_N + 1
@@ -43,7 +44,7 @@ def tile_multiscale_gcn_pa_t_kernel(
     nc = tc.nc
     with ExitStack() as ctx:
         const = ctx.enter_context(tc.tile_pool(name="const", bufs=1))
-        raw_pool = ctx.enter_context(tc.tile_pool(name="raw", bufs=4))
+        raw_pool = ctx.enter_context(tc.tile_pool(name="raw", bufs=5))
         grouped_pool = ctx.enter_context(tc.tile_pool(name="grouped", bufs=2))
         code_pool = ctx.enter_context(tc.tile_pool(name="codes", bufs=2))
         x_pool = ctx.enter_context(tc.tile_pool(name="x", bufs=2))
@@ -70,8 +71,8 @@ def tile_multiscale_gcn_pa_t_kernel(
 
         def load_feat(n, first_o):
             f_raw = f_raw_pool.tile([P, O_LOAD, SX, 2 * T], BF16)
-            for g in range(SG):
-                for x in range(SX):
+            for x in range(SX):
+                for g in (0, 2, 1, 3):
                     nc.sync.dma_start(
                         out=f_raw[WQ * g : WQ * (g + 1), :, x, :],
                         in_=feat[g + SG * x, n, first_o : first_o + O_LOAD, :, :].rearrange(
@@ -88,7 +89,9 @@ def tile_multiscale_gcn_pa_t_kernel(
                 in_=ada_w[SG * x : SG * (x + 1)].rearrange("g o i -> o g i"),
             )
         raws[1] = load_ada(1)
-        f_raws = {}
+        raws[2] = load_ada(2)
+        f_raws = {0: load_feat(0, 0)}
+        raws[3] = load_ada(3)
 
         b_raw = const.tile([SG, SX * COUT], BF16)
         nc.scalar.dma_start(
@@ -104,10 +107,8 @@ def tile_multiscale_gcn_pa_t_kernel(
         bn_raw = const.tile([P, 4, COUT], BF16)
         for i, vec in enumerate((bn_gamma, bn_beta, bn_mean, bn_var)):
             nc.scalar.dma_start(out=bn_raw[:, i, :], in_=vec.partition_broadcast(P))
-        res_sb = const.tile([P, N * COUT // 2, T], BF16)
-        nc.gpsimd.dma_start(
-            out=res_sb[:], in_=res.rearrange("n (a h) v t -> (h v) (n a) t", h=2)
-        )
+        res_sb = const.tile([P, N, COUT // 2, T], BF16)
+        res_view = res.rearrange("n (a h) v t -> (h v) n a t", h=2)
         out_view = out.rearrange("n (a h) v t -> (h v) n a t", h=2)
 
         ident = const.tile([P, P], F32)
@@ -154,9 +155,6 @@ def tile_multiscale_gcn_pa_t_kernel(
 
         def prepare_feat(group):
             per_load = O_LOAD // O_BANK
-            if group % per_load == 0:
-                n, bank = divmod(group, BANKS_N)
-                f_raws[group // per_load] = load_feat(n, O_BANK * bank)
             return regroup_feat(f_raws[group // per_load], O_BANK * (group % per_load))
 
         def quantise_feat(group, f_grouped):
@@ -333,18 +331,24 @@ def tile_multiscale_gcn_pa_t_kernel(
             nc.vector.tensor_add(
                 out=z[:],
                 in0=z[:],
-                in1=res_sb[:, (COUT // 2) * n + a0 : (COUT // 2) * n + a0 + O_BANK // 2, :],
+                in1=res_sb[:, n, a0 : a0 + O_BANK // 2, :],
             )
             nc.vector.tensor_scalar_max(out=z[:], in0=z[:], scalar1=0.0)
-            queue = nc.gpsimd if n == 0 else nc.sync
-            queue.dma_start(out=out_view[:, n, a0 : a0 + O_BANK // 2, :], in_=z[:])
+            nc.sync.dma_start(out=out_view[:, n, a0 : a0 + O_BANK // 2, :], in_=z[:])
 
         x_before = None
         unfinished = None
         for k in range(CHUNKS + 1):
             coming = k + AHEAD
+            if coming + EARLY < A_TILES:
+                raws[coming + EARLY] = load_ada(coming + EARLY)
+            if (k + EARLY) % (O_LOAD // O_BANK) == 0 and k + EARLY < N * BANKS_N:
+                n, bank = divmod(k + EARLY, BANKS_N)
+                f_raws[(k + EARLY) // (O_LOAD // O_BANK)] = load_feat(n, O_BANK * bank)
+            if k % CHUNKS_N == CHUNKS_N // 2:
+                n = k // CHUNKS_N
+                nc.sync.dma_start(out=res_sb[:, n, :, :], in_=res_view[:, n, :, :])
             if coming < A_TILES:
-                raws[coming] = load_ada(coming)
                 grouped = regroup_ada(raws[coming])
             if k < N * BANKS_N:
                 f_grouped = prepare_feat(k)

@@ -72,8 +72,9 @@ def tile_multiscale_gcn_pa_t_kernel(
         def load_feat(n, first_o):
             f_raw = f_raw_pool.tile([P, O_LOAD, SX, 2 * T], BF16)
             for x in range(SX):
-                for g in (0, 2, 1, 3):
-                    nc.sync.dma_start(
+                for g in range(SG):
+                    queue = nc.sync if g < SG // 2 else nc.gpsimd
+                    queue.dma_start(
                         out=f_raw[WQ * g : WQ * (g + 1), :, x, :],
                         in_=feat[g + SG * x, n, first_o : first_o + O_LOAD, :, :].rearrange(
                             "o (q e) t -> q o (e t)", e=2

@@ -31,11 +31,11 @@ CHUNKS_N = CHUNKS // N
 O_BANK = 8
 BANKS_N = COUT // O_BANK
 O_LOAD = 32
-AHEAD = 2
+AHEAD = 3
 EARLY = 2
 VECTOR_COLS = 448
 VECTOR_CHANNELS = 4
-F_LIVE = BANKS_N + 1
+F_LIVE = BANKS_N
 
 
 def tile_multiscale_gcn_pa_t_kernel(
@@ -44,7 +44,7 @@ def tile_multiscale_gcn_pa_t_kernel(
     nc = tc.nc
     with ExitStack() as ctx:
         const = ctx.enter_context(tc.tile_pool(name="const", bufs=1))
-        raw_pool = ctx.enter_context(tc.tile_pool(name="raw", bufs=5))
+        raw_pool = ctx.enter_context(tc.tile_pool(name="raw", bufs=4))
         grouped_pool = ctx.enter_context(tc.tile_pool(name="grouped", bufs=2))
         code_pool = ctx.enter_context(tc.tile_pool(name="codes", bufs=2))
         x_pool = ctx.enter_context(tc.tile_pool(name="x", bufs=2))
@@ -69,18 +69,15 @@ def tile_multiscale_gcn_pa_t_kernel(
             )
             return raw
 
-        def load_feat(n, first_o):
-            f_raw = f_raw_pool.tile([P, O_LOAD, SX, 2 * T], BF16)
+        def load_feat(f_raw, index, g):
+            n, part = divmod(index, COUT // O_LOAD)
             for x in range(SX):
-                for g in range(SG):
-                    queue = nc.sync if g < SG // 2 else nc.gpsimd
-                    queue.dma_start(
-                        out=f_raw[WQ * g : WQ * (g + 1), :, x, :],
-                        in_=feat[g + SG * x, n, first_o : first_o + O_LOAD, :, :].rearrange(
-                            "o (q e) t -> q o (e t)", e=2
-                        ),
-                    )
-            return f_raw
+                nc.sync.dma_start(
+                    out=f_raw[WQ * g : WQ * (g + 1), :, x, :],
+                    in_=feat[
+                        g + SG * x, n, O_LOAD * part : O_LOAD * (part + 1), :, :
+                    ].rearrange("o (q e) t -> q o (e t)", e=2),
+                )
 
         raws = {0: load_ada(0)}
         w_raw = raw_pool.tile([P, SG, CIN], BF16, tag="raw")
@@ -91,8 +88,6 @@ def tile_multiscale_gcn_pa_t_kernel(
             )
         raws[1] = load_ada(1)
         raws[2] = load_ada(2)
-        f_raws = {0: load_feat(0, 0)}
-        raws[3] = load_ada(3)
 
         b_raw = const.tile([SG, SX * COUT], BF16)
         nc.scalar.dma_start(
@@ -165,6 +160,11 @@ def tile_multiscale_gcn_pa_t_kernel(
             f_code_tiles[group] = (f_codes, f_scales)
 
         grouped_0 = regroup_ada(raws[0])
+        raws[3] = load_ada(3)
+        f_raw = f_raw_pool.tile([P, O_LOAD, SX, 2 * T], BF16)
+        f_raws = {0: f_raw}
+        for g in range(SG):
+            load_feat(f_raw, 0, g)
 
         w_words = w_raw[:].bitcast(F32).rearrange("m g (c p u) -> m g c u p", c=C_PASSES, u=2)
         w_grouped = grouped_pool.tile([P, A_COLS, PACK], BF16, tag="grouped", align_bytes=64)
@@ -189,6 +189,7 @@ def tile_multiscale_gcn_pa_t_kernel(
                     out=w_grouped_words[:, c, 2 * g_pair : 2 * g_pair + 2, :, :],
                     in_=w_turned[:].rearrange("p (g u) m -> p g m u", u=2),
                 )
+        raws[4] = load_ada(4)
         w_codes = const.tile([P, C_PASSES * SG * P], U32, align_bytes=64)
         w_scales = const.tile([P, C_PASSES * SG * P], U8, align_bytes=64)
 
@@ -215,6 +216,7 @@ def tile_multiscale_gcn_pa_t_kernel(
             in_=pa_turned[:, 0:2, :].rearrange("p e (x v) -> p v x e", x=SX),
         )
 
+        grouped = regroup_ada(raws[2])
         quantise_ada(1, grouped_1)
 
         bn_f = const.tile([P, 4, COUT], F32)
@@ -337,22 +339,26 @@ def tile_multiscale_gcn_pa_t_kernel(
             nc.vector.tensor_scalar_max(out=z[:], in0=z[:], scalar1=0.0)
             nc.sync.dma_start(out=out_view[:, n, a0 : a0 + O_BANK // 2, :], in_=z[:])
 
+        per_load = O_LOAD // O_BANK
         x_before = None
         unfinished = None
+        f_grouped = None
         for k in range(CHUNKS + 1):
-            coming = k + AHEAD
-            if coming + EARLY < A_TILES:
-                raws[coming + EARLY] = load_ada(coming + EARLY)
-            if (k + EARLY) % (O_LOAD // O_BANK) == 0 and k + EARLY < N * BANKS_N:
-                n, bank = divmod(k + EARLY, BANKS_N)
-                f_raws[(k + EARLY) // (O_LOAD // O_BANK)] = load_feat(n, O_BANK * bank)
+            if k + AHEAD + EARLY < A_TILES:
+                raws[k + AHEAD + EARLY] = load_ada(k + AHEAD + EARLY)
+            if k // per_load + 1 < N * BANKS_N // per_load:
+                if k % per_load == 0:
+                    f_raw = f_raw_pool.tile([P, O_LOAD, SX, 2 * T], BF16)
+                    f_raws[k // per_load + 1] = f_raw
+                load_feat(f_raws[k // per_load + 1], k // per_load + 1, k % per_load)
             if k % CHUNKS_N == CHUNKS_N // 2:
                 n = k // CHUNKS_N
                 nc.sync.dma_start(out=res_sb[:, n, :, :], in_=res_view[:, n, :, :])
-            if coming < A_TILES:
-                grouped = regroup_ada(raws[coming])
-            if k < N * BANKS_N:
-                f_grouped = prepare_feat(k)
+
+            if k + AHEAD - 1 < A_TILES:
+                quantise_ada(k + AHEAD - 1, grouped)
+            if k > 0:
+                quantise_feat(k - 1, f_grouped)
             if unfinished is not None:
                 finish(0, k - CHUNKS_N - 1, unfinished)
                 unfinished = None
@@ -367,10 +373,10 @@ def tile_multiscale_gcn_pa_t_kernel(
                 x_before = first_matmul(k)
             if CHUNKS_N <= k < CHUNKS:
                 unfinished = second_matmul(0, k - CHUNKS_N, a_codes2, a_scales2)
-            if coming < A_TILES:
-                quantise_ada(coming, grouped)
+            if k + AHEAD < A_TILES:
+                grouped = regroup_ada(raws[k + AHEAD])
             if k < N * BANKS_N:
-                quantise_feat(k, f_grouped)
+                f_grouped = prepare_feat(k)
 
         for bank in range(BANKS_N):
             z = second_matmul(1, bank, a_codes2, a_scales2)

from contextlib import ExitStack

import concourse.mybir as mybir
from concourse.masks import make_identity

F32 = mybir.dt.float32
BF16 = mybir.dt.bfloat16
U32 = mybir.dt.uint32
U8 = mybir.dt.uint8
FP8X4 = mybir.dt.float8_e4m3fn_x4
ACT = mybir.ActivationFunctionType
ALU = mybir.AluOpType

N, CIN, COUT, V, T, S = 2, 1024, 64, 64, 64, 8
EPS = 1e-5
FLOPS = 2 * N * S * COUT * CIN * V * V + 2 * N * COUT * V * S * V * T

P = 128
PACK = 4
K_PASS = P * PACK
C_PASSES = CIN // K_PASS
SG = 4
SX = 2
WQ = V // 2
A_COLS = 1024
A_TILES = N * C_PASSES * V * V // A_COLS
CHUNK = 512
V_CHUNK = CHUNK // V
CHUNKS = N * V * V // CHUNK
CHUNKS_N = CHUNKS // N
O_BANK = 8
BANKS_N = COUT // O_BANK
O_LOAD = 32
AHEAD = 3
EARLY = 2
VECTOR_COLS = 448
VECTOR_CHANNELS = 4
F_LIVE = BANKS_N


def tile_multiscale_gcn_pa_t_kernel(
    tc, ada_A, ada_w, ada_b, PA, feat, bn_gamma, bn_beta, bn_mean, bn_var, res, out
):
    nc = tc.nc
    with ExitStack() as ctx:
        const = ctx.enter_context(tc.tile_pool(name="const", bufs=1))
        raw_pool = ctx.enter_context(tc.tile_pool(name="raw", bufs=4))
        grouped_pool = ctx.enter_context(tc.tile_pool(name="grouped", bufs=2))
        code_pool = ctx.enter_context(tc.tile_pool(name="codes", bufs=2))
        x_pool = ctx.enter_context(tc.tile_pool(name="x", bufs=2))
        a_pool = ctx.enter_context(tc.tile_pool(name="a", bufs=1))
        f_raw_pool = ctx.enter_context(tc.tile_pool(name="f_raw", bufs=2))
        f_code_pool = ctx.enter_context(tc.tile_pool(name="f_codes", bufs=F_LIVE))
        z_pool = ctx.enter_context(tc.tile_pool(name="z", bufs=4))
        ps_mx = ctx.enter_context(tc.psum_pool(name="ps_mx", bufs=4))
        ps_turn = ctx.enter_context(tc.psum_pool(name="ps_turn", bufs=4))
        ctx.enter_context(tc.manual_schedule())

        def load_ada(index):
            quarter, c = divmod(index, C_PASSES)
            n, q = divmod(quarter, V * V // A_COLS)
            v0 = q * (A_COLS // V)
            raw = raw_pool.tile([P, PACK, A_COLS], BF16, tag="raw")
            nc.sync.dma_start(
                out=raw[:],
                in_=ada_A[
                    n, K_PASS * c : K_PASS * (c + 1), v0 : v0 + A_COLS // V, :
                ].rearrange("(p j) v w -> p j (v w)", j=PACK),
            )
            return raw

        def load_feat(f_raw, index, g):
            n, part = divmod(index, COUT // O_LOAD)
            for x in range(SX):
                nc.sync.dma_start(
                    out=f_raw[WQ * g : WQ * (g + 1), :, x, :],
                    in_=feat[
                        g + SG * x, n, O_LOAD * part : O_LOAD * (part + 1), :, :
                    ].rearrange("o (q e) t -> q o (e t)", e=2),
                )

        raws = {0: load_ada(0)}
        w_raw = raw_pool.tile([P, SG, CIN], BF16, tag="raw")
        for x in range(SX):
            nc.sync.dma_start(
                out=w_raw[COUT * x : COUT * (x + 1), :, :],
                in_=ada_w[SG * x : SG * (x + 1)].rearrange("g o i -> o g i"),
            )
        raws[1] = load_ada(1)
        raws[2] = load_ada(2)

        b_raw = const.tile([SG, SX * COUT], BF16)
        nc.scalar.dma_start(
            out=b_raw[:].rearrange("g (x o) -> g x o", x=SX),
            in_=ada_b.rearrange("(x g) o -> g x o", x=SX),
        )
        pa_raw = const.tile([P, SG * V], BF16)
        for x in range(SX):
            nc.scalar.dma_start(
                out=pa_raw[V * x : V * (x + 1), :].rearrange("v (g w) -> v g w", g=SG),
                in_=PA[SG * x : SG * (x + 1)].rearrange("g v w -> v g w"),
            )
        bn_raw = const.tile([P, 4, COUT], BF16)
        for i, vec in enumerate((bn_gamma, bn_beta, bn_mean, bn_var)):
            nc.scalar.dma_start(out=bn_raw[:, i, :], in_=vec.partition_broadcast(P))
        res_sb = const.tile([P, N, COUT // 2, T], BF16)
        res_view = res.rearrange("n (a h) v t -> (h v) n a t", h=2)
        out_view = out.rearrange("n (a h) v t -> (h v) n a t", h=2)

        ident = const.tile([P, P], F32)
        make_identity(nc, ident[:])

        def regroup_ada(raw):
            grouped = grouped_pool.tile([P, A_COLS, PACK], BF16, tag="grouped", align_bytes=64)
            dst = grouped[:].rearrange("p (c i) j -> p c j i", i=4)
            src = raw[:].rearrange("p j (c i) -> p c j i", i=4)
            cut = VECTOR_COLS // 4
            nc.vector.tensor_copy(out=dst[:, :cut], in_=src[:, :cut])
            nc.scalar.copy(out=dst[:, cut:], in_=src[:, cut:])
            return grouped

        def regroup_feat(f_raw, first_o):
            f_grouped = grouped_pool.tile([P, O_BANK * T, PACK], BF16, align_bytes=64)
            dst = f_grouped[:].rearrange("p (o t) j -> p o t j", t=T)
            src = f_raw[:, first_o : first_o + O_BANK, :, :].rearrange(
                "p o x (e t) -> p o t (x e)", e=2
            )
            cut = VECTOR_CHANNELS
            nc.vector.tensor_copy(out=dst[:, :cut], in_=src[:, :cut])
            nc.scalar.copy(out=dst[:, cut:], in_=src[:, cut:])
            return f_grouped

        def quantise(grouped, codes, scales):
            nc.vector.quantize_mx(
                out=codes.bitcast(FP8X4),
                scales=scales,
                in_=grouped[:].rearrange("p w j -> p (w j)"),
            )

        a_code_tiles = {}
        f_code_tiles = {}

        def quantise_ada(index, grouped):
            quarter, c = divmod(index, C_PASSES)
            if c == 0:
                a_codes = code_pool.tile([P, C_PASSES, A_COLS], U32, align_bytes=64)
                a_scales = code_pool.tile([P, C_PASSES, A_COLS], U8, align_bytes=64)
                a_code_tiles[quarter] = (a_codes, a_scales)
            a_codes, a_scales = a_code_tiles[quarter]
            quantise(grouped, a_codes[:, c, :], a_scales[:, c, :])

        def prepare_feat(group):
            per_load = O_LOAD // O_BANK
            return regroup_feat(f_raws[group // per_load], O_BANK * (group % per_load))

        def quantise_feat(group, f_grouped):
            f_codes = f_code_pool.tile([P, O_BANK * T], U32, align_bytes=64)
            f_scales = f_code_pool.tile([P, O_BANK * T], U8, align_bytes=64)
            quantise(f_grouped, f_codes[:], f_scales[:])
            f_code_tiles[group] = (f_codes, f_scales)

        grouped_0 = regroup_ada(raws[0])
        raws[3] = load_ada(3)
        f_raw = f_raw_pool.tile([P, O_LOAD, SX, 2 * T], BF16)
        f_raws = {0: f_raw}
        for g in range(SG):
            load_feat(f_raw, 0, g)

        w_words = w_raw[:].bitcast(F32).rearrange("m g (c p u) -> m g c u p", c=C_PASSES, u=2)
        w_grouped = grouped_pool.tile([P, A_COLS, PACK], BF16, tag="grouped", align_bytes=64)
        w_grouped_words = (
            w_grouped[:]
            .rearrange("p w j -> p (w j)")
            .bitcast(F32)
            .rearrange("p (c g m u) -> p c g m u", c=C_PASSES, g=SG, u=2)
        )
        for c in range(C_PASSES):
            for g_pair in range(SG // 2):
                w_turned = ps_turn.tile([P, 4, P], F32, tag="turned")
                for g_low in range(2):
                    for u in range(2):
                        nc.tensor.transpose(
                            w_turned[:, 2 * g_low + u, :],
                            w_words[:, 2 * g_pair + g_low, c, u, :],
                            ident[:],
                        )
                copy_out = nc.vector.tensor_copy if g_pair == 0 else nc.scalar.copy
                copy_out(
                    out=w_grouped_words[:, c, 2 * g_pair : 2 * g_pair + 2, :, :],
                    in_=w_turned[:].rearrange("p (g u) m -> p g m u", u=2),
                )
        raws[4] = load_ada(4)
        w_codes = const.tile([P, C_PASSES * SG * P], U32, align_bytes=64)
        w_scales = const.tile([P, C_PASSES * SG * P], U8, align_bytes=64)

        b_square = const.tile([P, P], F32)
        nc.vector.memset(b_square[:], 0.0)
        nc.vector.tensor_copy(out=b_square[0:SG, :], in_=b_raw[:])
        b_turned = ps_turn.tile([P, 4, P], F32, tag="turned")
        nc.tensor.transpose(b_turned[:, 0, :], b_square[:], ident[:])
        bias_col = const.tile([P, SG], F32)
        nc.vector.tensor_copy(out=bias_col[:], in_=b_turned[:, 0, 0:SG])

        quantise(w_grouped, w_codes[:], w_scales[:])
        quantise_ada(0, grouped_0)
        grouped_1 = regroup_ada(raws[1])

        pa_sorted = const.tile([P, 2, P], F32)
        nc.vector.tensor_copy(out=pa_sorted[:], in_=pa_raw[:].rearrange("p (k e) -> p e k", e=2))
        pa_turned = ps_turn.tile([P, 4, P], F32, tag="turned")
        for e in range(2):
            nc.tensor.transpose(pa_turned[:, e, :], pa_sorted[:, e, :], ident[:])
        pa_t = const.tile([P, V, PACK], F32)
        nc.vector.tensor_copy(
            out=pa_t[:].rearrange("p v (x e) -> p v x e", x=SX),
            in_=pa_turned[:, 0:2, :].rearrange("p e (x v) -> p v x e", x=SX),
        )

        grouped = regroup_ada(raws[2])
        quantise_ada(1, grouped_1)

        bn_f = const.tile([P, 4, COUT], F32)
        nc.vector.tensor_copy(out=bn_f[:], in_=bn_raw[:])
        rstd = const.tile([P, COUT], F32)
        nc.vector.tensor_scalar_add(out=rstd[:], in0=bn_f[:, 3, :], scalar1=EPS)
        nc.scalar.activation(out=rstd[:], in_=rstd[:], func=ACT.Sqrt)
        nc.vector.reciprocal(out=rstd[:], in_=rstd[:])
        scale_all = const.tile([P, COUT], F32)
        nc.vector.tensor_mul(out=scale_all[:], in0=bn_f[:, 0, :], in1=rstd[:])
        shift_all = const.tile([P, COUT], F32)
        nc.vector.tensor_mul(out=shift_all[:], in0=bn_f[:, 2, :], in1=scale_all[:])
        nc.vector.tensor_sub(out=shift_all[:], in0=bn_f[:, 1, :], in1=shift_all[:])
        scale_col = const.tile([P, COUT // 2], F32)
        shift_col = const.tile([P, COUT // 2], F32)
        for h in range(2):
            rows = slice(V * h, V * (h + 1))
            nc.vector.tensor_copy(
                out=scale_col[rows, :],
                in_=scale_all[rows, :].rearrange("p (a h) -> p h a", h=2)[:, h, :],
            )
            nc.vector.tensor_copy(
                out=shift_col[rows, :],
                in_=shift_all[rows, :].rearrange("p (a h) -> p h a", h=2)[:, h, :],
            )

        def first_matmul(chunk):
            a_codes, a_scales = a_code_tiles[chunk // 2]
            cols = slice(CHUNK * (chunk % 2), CHUNK * (chunk % 2 + 1))
            x_sb = x_pool.tile([P, V_CHUNK, 2, SG, WQ], F32)
            for g in range(SG):
                acc = ps_mx.tile([P, CHUNK], F32, tag="mx")
                for c in range(C_PASSES):
                    w_cols = slice(P * (SG * c + g), P * (SG * c + g + 1))
                    nc.tensor.matmul_mx(
                        out=acc[:],
                        lhsT=w_codes[:, w_cols].bitcast(FP8X4),
                        lhsT_scale=w_scales[:, w_cols],
                        rhs=a_codes[:, c, cols].bitcast(FP8X4),
                        rhs_scale=a_scales[:, c, cols],
                        start=(c == 0),
                        stop=(c == C_PASSES - 1),
                    )
                nc.scalar.activation(
                    out=x_sb[:, :, :, g, :],
                    in_=acc[:].rearrange("p (v q e) -> p v e q", v=V_CHUNK, e=2),
                    func=ACT.Identity,
                    bias=bias_col[:, g : g + 1],
                    scale=1.0,
                )
            return x_sb

        def turn_and_modulate(x_sb, a_in, first_v):
            for pair in range(V_CHUNK // 2):
                turned = ps_turn.tile([P, 2, SX, 2, COUT], F32, tag="turned")
                for dv in range(2):
                    for e in range(2):
                        nc.tensor.transpose(
                            turned[:, dv, :, e, :],
                            x_sb[:, 2 * pair + dv, e, :, :].rearrange("p g q -> p (g q)"),
                            ident[:],
                        )
                v0 = first_v + 2 * pair
                nc.vector.tensor_tensor(
                    out=a_in[:, :, v0 : v0 + 2, :],
                    in0=turned[:].rearrange("p v x e o -> p o v (x e)"),
                    in1=pa_t[:, v0 : v0 + 2, :].unsqueeze(1).to_broadcast([P, COUT, 2, PACK]),
                    op=ALU.mult,
                )

        def quantise_a(a_in):
            a_codes2 = a_pool.tile([P, COUT * V], U32, align_bytes=64)
            a_scales2 = a_pool.tile([P, COUT * V], U8, align_bytes=64)
            width = O_BANK * V
            for bank in range(BANKS_N):
                nc.vector.quantize_mx(
                    out=a_codes2[:, width * bank : width * (bank + 1)].bitcast(FP8X4),
                    scales=a_scales2[:, width * bank : width * (bank + 1)],
                    in_=a_in[:, O_BANK * bank : O_BANK * (bank + 1), :, :].rearrange(
                        "p o v j -> p (o v j)"
                    ),
                )
            return a_codes2, a_scales2

        def second_matmul(n, bank, a_codes2, a_scales2):
            f_codes, f_scales = f_code_tiles[BANKS_N * n + bank]
            y_ps = ps_mx.tile([P, O_BANK // 2, P], F32, tag="mx")
            z = z_pool.tile([P, O_BANK // 2, T], F32)
            for pair in range(O_BANK // 2):
                a = (O_BANK // 2) * bank + pair
                nc.tensor.matmul_mx(
                    out=y_ps[:, pair, :],
                    lhsT=a_codes2[:, P * a : P * (a + 1)].bitcast(FP8X4),
                    lhsT_scale=a_scales2[:, P * a : P * (a + 1)],
                    rhs=f_codes[:, P * pair : P * (pair + 1)].bitcast(FP8X4),
                    rhs_scale=f_scales[:, P * pair : P * (pair + 1)],
                    start=True,
                    stop=True,
                )
            for pair in range(O_BANK // 2):
                a = (O_BANK // 2) * bank + pair
                for h in range(2):
                    rows = slice(V * h, V * (h + 1))
                    nc.scalar.activation(
                        out=z[rows, pair, :],
                        in_=y_ps[rows, pair, T * h : T * (h + 1)],
                        func=ACT.Identity,
                        bias=shift_col[rows, a : a + 1],
                        scale=scale_col[rows, a : a + 1],
                    )
            return z

        def finish(n, bank, z):
            a0 = (O_BANK // 2) * bank
            nc.vector.tensor_add(
                out=z[:],
                in0=z[:],
                in1=res_sb[:, n, a0 : a0 + O_BANK // 2, :],
            )
            nc.vector.tensor_scalar_max(out=z[:], in0=z[:], scalar1=0.0)
            nc.sync.dma_start(out=out_view[:, n, a0 : a0 + O_BANK // 2, :], in_=z[:])

        per_load = O_LOAD // O_BANK
        x_before = None
        unfinished = None
        f_grouped = None
        for k in range(CHUNKS + 1):
            if k + AHEAD + EARLY < A_TILES:
                raws[k + AHEAD + EARLY] = load_ada(k + AHEAD + EARLY)
            if k // per_load + 1 < N * BANKS_N // per_load:
                if k % per_load == 0:
                    f_raw = f_raw_pool.tile([P, O_LOAD, SX, 2 * T], BF16)
                    f_raws[k // per_load + 1] = f_raw
                load_feat(f_raws[k // per_load + 1], k // per_load + 1, k % per_load)
            if k % CHUNKS_N == CHUNKS_N // 2:
                n = k // CHUNKS_N
                nc.sync.dma_start(out=res_sb[:, n, :, :], in_=res_view[:, n, :, :])

            if k + AHEAD - 1 < A_TILES:
                quantise_ada(k + AHEAD - 1, grouped)
            if k > 0:
                quantise_feat(k - 1, f_grouped)
            if unfinished is not None:
                finish(0, k - CHUNKS_N - 1, unfinished)
                unfinished = None
            if k > 0:
                n, chunk = divmod(k - 1, CHUNKS_N)
                if chunk == 0:
                    a_in = a_pool.tile([P, COUT, V, PACK], BF16, align_bytes=64)
                turn_and_modulate(x_before, a_in, V_CHUNK * chunk)
                if chunk == CHUNKS_N - 1:
                    a_codes2, a_scales2 = quantise_a(a_in)
            if k < CHUNKS:
                x_before = first_matmul(k)
            if CHUNKS_N <= k < CHUNKS:
                unfinished = second_matmul(0, k - CHUNKS_N, a_codes2, a_scales2)
            if k + AHEAD < A_TILES:
                grouped = regroup_ada(raws[k + AHEAD])
            if k < N * BANKS_N:
                f_grouped = prepare_feat(k)

        for bank in range(BANKS_N):
            z = second_matmul(1, bank, a_codes2, a_scales2)
            if bank > 0:
                finish(1, bank - 1, unfinished)
            unfinished = z
        finish(1, BANKS_N - 1, unfinished)
